import numpy as np
import ml_dtypes


def mxq(x, axis, fmt="e4m3"):
    dtype, down = {"e4m3": (ml_dtypes.float8_e4m3fn, 7), "e5m2": (ml_dtypes.float8_e5m2, 14)}[fmt]
    v = np.moveaxis(np.asarray(x, np.float32).astype(ml_dtypes.bfloat16).astype(np.float64), axis, -1)
    blocks = v.reshape(v.shape[:-1] + (-1, 32))
    amax = np.abs(blocks).max(-1, keepdims=True)
    byte = np.maximum(np.where(amax > 0, np.frexp(amax)[1] - 1 + 127, 0) - down, 1)
    scale = np.exp2(byte - 127.0)
    codes = (blocks / scale).astype(np.float32).astype(dtype).astype(np.float64)
    return np.moveaxis((codes * scale).reshape(v.shape), -1, axis)


WIDE = False


def mx_kscale(k):
    if not WIDE:
        return np.ones(k)
    levels = np.array([10, -10, 5, -5, 0])
    if k % 512:
        return np.exp2(np.random.permutation(np.resize(levels, k // 32))).repeat(32)
    a = np.empty((k // 512, 16))
    for p in range(k // 512):
        a[p, :8] = np.random.permutation(np.resize(levels, 8))
        for g in range(8):
            far = levels[np.abs(levels - a[p, g]) >= 10]
            a[p, g + 8] = far[np.random.randint(len(far))]
    return np.exp2(a.ravel()).repeat(32)


BF16 = ml_dtypes.bfloat16


def bf(x):
    return np.asarray(x, np.float32).astype(BF16)


def f64(x):
    return np.asarray(x).astype(np.float64)


B, N, DIM, H, D, M = 4, 2048, 512, 2, 64, 16
HD = H * D
HALF = D // 2
EPS = 1e-12


def l2norm(t):
    n = np.sqrt((t * t).sum(-1, keepdims=True))
    return t / np.maximum(n, EPS)


def rope(t, fr):
    rot = np.concatenate([-t[..., HALF:], t[..., :HALF]], axis=-1)
    return t * np.cos(fr) + rot * np.sin(fr)


def heads(t):
    return t.reshape(B, N, H, D).transpose(0, 2, 1, 3)


def setup_inputs():
    s = mx_kscale(DIM)
    ang = np.random.uniform(-np.pi, np.pi, (N, HALF))
    return {"x": bf(np.random.standard_normal((B, N, DIM)) * s),
            "freqs": bf(np.concatenate([ang, ang], axis=-1)),
            "Wq": bf(np.random.standard_normal((DIM, HD)) / np.sqrt(DIM) / s[:, None]),
            "Wk": bf(np.random.standard_normal((DIM, HD)) / np.sqrt(DIM) / s[:, None]),
            "Wv": bf(np.random.standard_normal((DIM, HD)) / np.sqrt(DIM) / s[:, None]),
            "mem_k": bf(np.random.standard_normal((H, M, D))),
            "mem_v": bf(np.random.standard_normal((H, M, D)))}


def reference(x, freqs, Wq, Wk, Wv, mem_k, mem_v):
    xq = mxq(f64(x), 2, "e4m3")
    fr = f64(freqs)
    q = heads(xq @ mxq(f64(Wq), 0, "e4m3"))
    k = heads(xq @ mxq(f64(Wk), 0, "e4m3"))
    v = heads(xq @ mxq(f64(Wv), 0, "e4m3"))
    q = rope(l2norm(q), fr)
    k = rope(l2norm(k), fr)
    v = rope(v, fr)
    mk = np.broadcast_to(l2norm(f64(mem_k))[None], (B, H, M, D))
    mv = np.broadcast_to(f64(mem_v)[None], (B, H, M, D))
    return q, np.concatenate([mk, k], axis=2), np.concatenate([mv, v], axis=2)

@@ -1,0 +1,312 @@
+from contextlib import ExitStack
+
+import concourse.mybir as mybir
+from concourse.masks import make_identity
+
+F32 = mybir.dt.float32
+BF16 = mybir.dt.bfloat16
+I32 = mybir.dt.int32
+U32 = mybir.dt.uint32
+U8 = mybir.dt.uint8
+FP8X4 = mybir.dt.float8_e4m3fn_x4
+ACT = mybir.ActivationFunctionType
+ALU = mybir.AluOpType
+
+P = 128
+BATCH, TOKENS, DIM = 4, 2048, 512
+HEADS, HEAD_DIM, MEM = 2, 64, 16
+HALF = HEAD_DIM // 2
+HEAD_GROUPS = 3 * HEADS
+NORMED = 2 * HEADS
+COLS = HEAD_GROUPS * HEAD_DIM
+PASS_COLS = 512
+ROW_TILES = TOKENS // P
+GROUP = 4
+GROUPS_PER_BATCH = ROW_TILES // GROUP
+N_GROUPS = BATCH * GROUPS_PER_BATCH
+EPS = 1e-12
+
+PREPARE_AHEAD = 2
+QUANTISE_AHEAD = 1
+NORMALISE_BEHIND = 2
+
+FLOPS = 2 * BATCH * TOKENS * DIM * COLS
+
+
+def quantise_weights(nc, const, w_rows):
+    w_grouped = const.tile([P, PASS_COLS, 4], BF16, align_bytes=64)
+    nc.vector.memset(w_grouped[:].bitcast(I32)[:, COLS:PASS_COLS, :], 0)
+    dst = w_grouped[:, 0:COLS, :].rearrange("p (a w h i) t -> p a w h i t", a=2, w=3, h=HEADS)
+    for w in range(3):
+        src = w_rows[:, w].rearrange("p t (h a i) -> p a h i t", h=HEADS, a=2)
+        for a in range(2):
+            nc.vector.tensor_copy(out=dst[:, a, w], in_=src[:, a])
+    w_codes = const.tile([P, PASS_COLS], U32, align_bytes=64)
+    w_scales = const.tile([P, PASS_COLS], U8, align_bytes=64)
+    nc.vector.quantize_mx(
+        out=w_codes[:].bitcast(FP8X4),
+        scales=w_scales[:],
+        in_=w_grouped[:].rearrange("p c t -> p (c t)"),
+    )
+    return w_codes, w_scales
+
+
+def tile_attention_pa_t_kernel(
+    tc, x, freqs, Wq, Wk, Wv, mem_k, mem_v, out_0, out_1, out_2
+):
+    nc = tc.nc
+    with ExitStack() as ctx:
+        ctx.enter_context(tc.manual_schedule())
+        const = ctx.enter_context(tc.tile_pool(name="const", bufs=1))
+        x_pool = ctx.enter_context(tc.tile_pool(name="x", bufs=N_GROUPS))
+        quant = ctx.enter_context(tc.tile_pool(name="quant", bufs=3))
+        norms = ctx.enter_context(tc.tile_pool(name="norms", bufs=5))
+        scratch = ctx.enter_context(tc.tile_pool(name="scratch", bufs=2))
+        products_pool = ctx.enter_context(tc.tile_pool(name="products", bufs=3))
+        result_pool = ctx.enter_context(tc.tile_pool(name="result", bufs=6))
+        psum_xt = ctx.enter_context(tc.psum_pool(name="psum_xt", bufs=3))
+        psum_t = ctx.enter_context(tc.psum_pool(name="psum_t", bufs=5))
+
+        mem_rows = HEADS * MEM
+        mk = const.tile([mem_rows, HEAD_DIM], BF16)
+        nc.sync.dma_start(out=mk[:], in_=mem_k.rearrange("h m d -> (h m) d"))
+        mv = const.tile([mem_rows, HEAD_DIM], BF16)
+        nc.sync.dma_start(out=mv[:], in_=mem_v.rearrange("h m d -> (h m) d"))
+        w_rows = const.tile([P, 3, 4, P], BF16)
+        for w, weight in enumerate([Wq, Wk, Wv]):
+            nc.sync.dma_start(
+                out=w_rows[:, w],
+                in_=weight.rearrange("(p t) c -> p t c", t=4),
+            )
+        angle = const.tile([P, ROW_TILES, 2, HALF], BF16)
+        nc.sync.dma_start(
+            out=angle[:], in_=freqs.rearrange("(p j) (s i) -> p j s i", j=ROW_TILES, s=2)
+        )
+        x_groups = []
+        for b in range(BATCH):
+            x_rows = x[b].rearrange("(p j) k -> p j k", j=ROW_TILES)
+            for c in range(GROUPS_PER_BATCH):
+                x_group = x_pool.tile([P, GROUP, DIM], BF16)
+                nc.sync.dma_start(out=x_group[:], in_=x_rows[:, c * GROUP : (c + 1) * GROUP, :])
+                x_groups.append(x_group)
+
+        identity = const.tile([P, P], F32)
+        make_identity(nc, identity[:])
+
+        floor = const.tile([P, 1], F32)
+        nc.vector.memset(floor[:], EPS * EPS)
+        minus_floor = const.tile([P, 1], F32)
+        nc.vector.memset(minus_floor[:], -EPS * EPS)
+
+        mv_out = const.tile([mem_rows, BATCH, HEAD_DIM], F32)
+        nc.gpsimd.tensor_copy(
+            out=mv_out[:], in_=mv[:].unsqueeze(1).to_broadcast([mem_rows, BATCH, HEAD_DIM])
+        )
+        mk_squares = const.tile([mem_rows, HEAD_DIM], F32)
+        mk_sum = const.tile([mem_rows, 1], F32)
+        nc.scalar.activation(out=mk_squares[:], in_=mk[:], func=ACT.Square, accum_out=mk_sum[:])
+        mk_excess = const.tile([mem_rows, 1], F32)
+        nc.scalar.activation(
+            out=mk_excess[:], in_=mk_sum[:], func=ACT.Relu, bias=minus_floor[0:mem_rows]
+        )
+
+        def finish_memory_rows():
+            mk_rnorm = const.tile([mem_rows, 1], F32)
+            nc.scalar.activation(
+                out=mk_rnorm[:],
+                in_=mk_excess[:],
+                func=ACT.Abs_reciprocal_sqrt,
+                bias=floor[0:mem_rows],
+            )
+            mk_out = const.tile([mem_rows, BATCH, HEAD_DIM], F32)
+            nc.scalar.activation(
+                out=mk_out[:],
+                in_=mk[:].unsqueeze(1).to_broadcast([mem_rows, BATCH, HEAD_DIM]),
+                func=ACT.Copy,
+                scale=mk_rnorm[:],
+            )
+            for h in range(HEADS):
+                slots = slice(h * MEM, (h + 1) * MEM)
+                nc.sync.dma_start(
+                    out=out_1[:, h, 0:MEM, :].rearrange("b m d -> m b d"), in_=mk_out[slots]
+                )
+                nc.sync.dma_start(
+                    out=out_2[:, h, 0:MEM, :].rearrange("b m d -> m b d"), in_=mv_out[slots]
+                )
+
+        w_codes, w_scales = quantise_weights(nc, const, w_rows)
+
+        table = const.tile([P, ROW_TILES, 4, HALF], F32)
+
+        grouped_of, codes_of, scales_of = {}, {}, {}
+        sums_of, excess_of, rnorm_of = {}, {}, {}
+        squares_of, products_of, result_of = {}, {}, {}
+
+        def table_rows(g):
+            js = slice(g * GROUP, (g + 1) * GROUP)
+            half_sine = scratch.tile([P, GROUP, 2, HALF], F32)
+            nc.scalar.activation(out=half_sine[:], in_=angle[:, js], func=ACT.Sin, scale=0.5)
+            nc.scalar.activation(
+                out=table[:, js, 1, :], in_=angle[:, js, 1, :], func=ACT.Sin, scale=1.0
+            )
+            nc.scalar.activation(
+                out=table[:, js, 2, :], in_=angle[:, js, 0, :], func=ACT.Sin, scale=-1.0
+            )
+            half_sine_squared = scratch.tile([P, GROUP, 2, HALF], F32)
+            nc.gpsimd.tensor_tensor(
+                out=half_sine_squared[:], in0=half_sine[:], in1=half_sine[:], op=ALU.mult
+            )
+            nc.gpsimd.tensor_scalar(
+                out=table[:, js, 0:4:3, :],
+                in0=half_sine_squared[:],
+                scalar1=-2.0,
+                scalar2=1.0,
+                op0=ALU.mult,
+                op1=ALU.add,
+            )
+
+        def prepare(g):
+            x_words = x_groups[g][:].bitcast(F32)
+            grouped = quant.tile([P, GROUP, P, 4], BF16, align_bytes=64)
+            grouped_of[g] = grouped
+            grouped_words = grouped[:].bitcast(F32)
+            for pair in range(GROUP // 2):
+                xt = psum_xt.tile([P, 2, 2, P], F32)
+                for s in range(2):
+                    for u in range(2):
+                        nc.tensor.transpose(
+                            out=xt[:, s, u, :],
+                            in_=x_words[:, 2 * pair + s, u : 2 * P : 2],
+                            identity=identity[:],
+                        )
+                nc.scalar.copy(
+                    out=grouped_words[:, 2 * pair : 2 * pair + 2],
+                    in_=xt[:].rearrange("p s u r -> p s r u"),
+                )
+
+        def quantise(g):
+            x_codes = quant.tile([P, GROUP * P], U32, align_bytes=64)
+            x_scales = quant.tile([P, GROUP * P], U8, align_bytes=64)
+            codes_of[g], scales_of[g] = x_codes, x_scales
+            nc.vector.quantize_mx(
+                out=x_codes[:].bitcast(FP8X4),
+                scales=x_scales[:],
+                in_=grouped_of[g][:].rearrange("p s r t -> p (s r t)"),
+            )
+
+        def open_group(g):
+            squares = scratch.tile([P, GROUP, NORMED, 2, HALF], F32)
+            sums = norms.tile([P, GROUP, NORMED], F32)
+            products = products_pool.tile([P, GROUP, 2 * COLS], F32)
+            result = result_pool.tile([P, HEAD_GROUPS, GROUP, HEAD_DIM], F32)
+            squares_of[g], sums_of[g], products_of[g], result_of[g] = squares, sums, products, result
+
+        def project(g, s):
+            tokens = slice(s * P, (s + 1) * P)
+            t_psum = psum_t.tile([P, PASS_COLS], F32)
+            nc.tensor.matmul_mx(
+                out=t_psum[:],
+                lhsT=codes_of[g][:, tokens].bitcast(FP8X4),
+                lhsT_scale=scales_of[g][:, tokens],
+                rhs=w_codes[:].bitcast(FP8X4),
+                rhs_scale=w_scales[:],
+                start=True,
+                stop=True,
+            )
+            t_halves = t_psum[:, 0:COLS].rearrange("p (a g i) -> p a g i", a=2, g=HEAD_GROUPS)
+            for n in range(NORMED):
+                nc.scalar.activation(
+                    out=squares_of[g][:, s, n],
+                    in_=t_halves[:, :, n, :],
+                    func=ACT.Square,
+                    accum_out=sums_of[g][:, s, n : n + 1],
+                )
+            j = (g % GROUPS_PER_BATCH) * GROUP + s
+            shape = [P, 2, 2, HEAD_GROUPS, HALF]
+            nc.vector.tensor_tensor(
+                out=products_of[g][:, s, :].rearrange(
+                    "p (a r g i) -> p a r g i", a=2, r=2, g=HEAD_GROUPS
+                ),
+                in0=t_halves.unsqueeze(2).to_broadcast(shape),
+                in1=table[:, j].rearrange("p (a r) i -> p a r i", a=2).unsqueeze(3).to_broadcast(shape),
+                op=ALU.mult,
+            )
+
+        def add_products(engine, g, tiles):
+            by_source = products_of[g][:, tiles, :].rearrange(
+                "p s (a r g i) -> p a s r g i", a=2, r=2, g=HEAD_GROUPS
+            )
+            engine.tensor_tensor(
+                out=result_of[g][:, :, tiles, :].rearrange("p g s (r i) -> p s r g i", r=2),
+                in0=by_source[:, 0],
+                in1=by_source[:, 1],
+                op=ALU.add,
+            )
+
+        def clamp_sums(g):
+            excess = norms.tile([P, GROUP, NORMED], F32)
+            excess_of[g] = excess
+            nc.scalar.activation(
+                out=excess[:], in_=sums_of[g][:], func=ACT.Relu, bias=minus_floor[:]
+            )
+
+        def root_sums(g):
+            rnorm = norms.tile([P, GROUP, NORMED], F32)
+            rnorm_of[g] = rnorm
+            nc.scalar.activation(
+                out=rnorm[:], in_=excess_of[g][:], func=ACT.Abs_reciprocal_sqrt, bias=floor[:]
+            )
+
+        def normalise(g, s):
+            for n in range(NORMED):
+                nc.scalar.activation(
+                    out=result_of[g][:, n, s, :],
+                    in_=result_of[g][:, n, s, :],
+                    func=ACT.Copy,
+                    scale=rnorm_of[g][:, s, n : n + 1],
+                )
+
+        def store(g):
+            b, j0 = g // GROUPS_PER_BATCH, (g % GROUPS_PER_BATCH) * GROUP
+            out_rows = [out_0[b], out_1[b, :, MEM:, :], out_2[b, :, MEM:, :]]
+            for w in range(3):
+                nc.sync.dma_start(
+                    out=out_rows[w].rearrange("h (p j) d -> p h j d", j=ROW_TILES)[
+                        :, :, j0 : j0 + GROUP, :
+                    ],
+                    in_=result_of[g][:, w * HEADS : (w + 1) * HEADS],
+                )
+
+        def live(g):
+            return 0 <= g < N_GROUPS
+
+        def pipeline_step(step):
+            if live(step - NORMALISE_BEHIND):
+                root_sums(step - NORMALISE_BEHIND)
+            if live(step + QUANTISE_AHEAD):
+                quantise(step + QUANTISE_AHEAD)
+            if live(step + PREPARE_AHEAD):
+                if step + PREPARE_AHEAD < GROUPS_PER_BATCH:
+                    table_rows(step + PREPARE_AHEAD)
+                prepare(step + PREPARE_AHEAD)
+            if live(step):
+                open_group(step)
+            for s in range(GROUP):
+                if live(step):
+                    project(step, s)
+                    if step == N_GROUPS - 1 and s % 2 == 1:
+                        add_products(nc.vector, step, slice(s - 1, s + 1))
+                if live(step - NORMALISE_BEHIND):
+                    normalise(step - NORMALISE_BEHIND, s)
+            if live(step):
+                clamp_sums(step)
+                if step < N_GROUPS - 1:
+                    add_products(nc.gpsimd, step, slice(0, GROUP))
+            if live(step - NORMALISE_BEHIND):
+                store(step - NORMALISE_BEHIND)
+
+        for step in range(-PREPARE_AHEAD, NORMALISE_BEHIND):
+            pipeline_step(step)
+        finish_memory_rows()
+        for step in range(NORMALISE_BEHIND, N_GROUPS + NORMALISE_BEHIND):
+            pipeline_step(step)

@@ -11,6 +11,7 @@ U8 = mybir.dt.uint8
 FP8X4 = mybir.dt.float8_e4m3fn_x4
 ACT = mybir.ActivationFunctionType
 ALU = mybir.AluOpType
+AXES = mybir.AxisListType
 
 P = 128
 BATCH, TOKENS, DIM = 4, 2048, 512
@@ -22,33 +23,13 @@ COLS = HEAD_GROUPS * HEAD_DIM
 PASS_COLS = 512
 ROW_TILES = TOKENS // P
 GROUP = 4
+PAIR = 2
 GROUPS_PER_BATCH = ROW_TILES // GROUP
 N_GROUPS = BATCH * GROUPS_PER_BATCH
+FOLD = 8
 EPS = 1e-12
 
-PREPARE_AHEAD = 2
-QUANTISE_AHEAD = 1
-NORMALISE_BEHIND = 2
-
 FLOPS = 2 * BATCH * TOKENS * DIM * COLS
-
-
-def quantise_weights(nc, const, w_rows):
-    w_grouped = const.tile([P, PASS_COLS, 4], BF16, align_bytes=64)
-    nc.vector.memset(w_grouped[:].bitcast(I32)[:, COLS:PASS_COLS, :], 0)
-    dst = w_grouped[:, 0:COLS, :].rearrange("p (a w h i) t -> p a w h i t", a=2, w=3, h=HEADS)
-    for w in range(3):
-        src = w_rows[:, w].rearrange("p t (h a i) -> p a h i t", h=HEADS, a=2)
-        for a in range(2):
-            nc.vector.tensor_copy(out=dst[:, a, w], in_=src[:, a])
-    w_codes = const.tile([P, PASS_COLS], U32, align_bytes=64)
-    w_scales = const.tile([P, PASS_COLS], U8, align_bytes=64)
-    nc.vector.quantize_mx(
-        out=w_codes[:].bitcast(FP8X4),
-        scales=w_scales[:],
-        in_=w_grouped[:].rearrange("p c t -> p (c t)"),
-    )
-    return w_codes, w_scales
 
 
 def tile_attention_pa_t_kernel(
@@ -60,150 +41,155 @@ def tile_attention_pa_t_kernel(
         const = ctx.enter_context(tc.tile_pool(name="const", bufs=1))
         x_pool = ctx.enter_context(tc.tile_pool(name="x", bufs=N_GROUPS))
         quant = ctx.enter_context(tc.tile_pool(name="quant", bufs=3))
-        norms = ctx.enter_context(tc.tile_pool(name="norms", bufs=5))
+        norms = ctx.enter_context(tc.tile_pool(name="norms", bufs=4))
         scratch = ctx.enter_context(tc.tile_pool(name="scratch", bufs=2))
         products_pool = ctx.enter_context(tc.tile_pool(name="products", bufs=3))
         result_pool = ctx.enter_context(tc.tile_pool(name="result", bufs=6))
-        psum_xt = ctx.enter_context(tc.psum_pool(name="psum_xt", bufs=3))
+        psum_xt = ctx.enter_context(tc.psum_pool(name="psum_xt", bufs=2))
         psum_t = ctx.enter_context(tc.psum_pool(name="psum_t", bufs=5))
+        psum_sum = ctx.enter_context(tc.psum_pool(name="psum_sum", bufs=1))
 
-        mem_rows = HEADS * MEM
-        mk = const.tile([mem_rows, HEAD_DIM], BF16)
-        nc.sync.dma_start(out=mk[:], in_=mem_k.rearrange("h m d -> (h m) d"))
-        mv = const.tile([mem_rows, HEAD_DIM], BF16)
-        nc.sync.dma_start(out=mv[:], in_=mem_v.rearrange("h m d -> (h m) d"))
         w_rows = const.tile([P, 3, 4, P], BF16)
         for w, weight in enumerate([Wq, Wk, Wv]):
-            nc.sync.dma_start(
-                out=w_rows[:, w],
-                in_=weight.rearrange("(p t) c -> p t c", t=4),
-            )
+            nc.sync.dma_start(out=w_rows[:, w], in_=weight.rearrange("(p t) c -> p t c", t=4))
         angle = const.tile([P, ROW_TILES, 2, HALF], BF16)
-        nc.sync.dma_start(
-            out=angle[:], in_=freqs.rearrange("(p j) (s i) -> p j s i", j=ROW_TILES, s=2)
-        )
+        mem_rows = HEADS * MEM
+        mk = const.tile([mem_rows, HEAD_DIM], BF16)
+        mv = const.tile([mem_rows, HEAD_DIM], BF16)
         x_groups = []
-        for b in range(BATCH):
+        for g in range(N_GROUPS):
+            b, j0 = g // GROUPS_PER_BATCH, (g % GROUPS_PER_BATCH) * GROUP
             x_rows = x[b].rearrange("(p j) k -> p j k", j=ROW_TILES)
-            for c in range(GROUPS_PER_BATCH):
-                x_group = x_pool.tile([P, GROUP, DIM], BF16)
-                nc.sync.dma_start(out=x_group[:], in_=x_rows[:, c * GROUP : (c + 1) * GROUP, :])
-                x_groups.append(x_group)
-
-        identity = const.tile([P, P], F32)
-        make_identity(nc, identity[:])
+            x_group = x_pool.tile([P, GROUP, DIM], BF16)
+            x_groups.append(x_group)
+            width = PAIR if g == 0 else GROUP
+            for c in range(0, GROUP, width):
+                nc.sync.dma_start(
+                    out=x_group[:, c : c + width], in_=x_rows[:, j0 + c : j0 + c + width, :]
+                )
+                if g == 0 and c == 0:
+                    nc.sync.dma_start(
+                        out=angle[:],
+                        in_=freqs.rearrange("(p j) (s i) -> p j s i", j=ROW_TILES, s=2),
+                    )
+            if g == 1:
+                nc.sync.dma_start(out=mk[:], in_=mem_k.rearrange("h m d -> (h m) d"))
+                nc.sync.dma_start(out=mv[:], in_=mem_v.rearrange("h m d -> (h m) d"))
 
         floor = const.tile([P, 1], F32)
         nc.vector.memset(floor[:], EPS * EPS)
         minus_floor = const.tile([P, 1], F32)
         nc.vector.memset(minus_floor[:], -EPS * EPS)
+        warm = const.tile([P, 2], F32)
+        nc.vector.memset(warm[:], 1.0)
+        nc.scalar.activation(out=warm[:, 0:1], in_=warm[:, 1:2], func=ACT.Sin)
 
-        mv_out = const.tile([mem_rows, BATCH, HEAD_DIM], F32)
-        nc.gpsimd.tensor_copy(
-            out=mv_out[:], in_=mv[:].unsqueeze(1).to_broadcast([mem_rows, BATCH, HEAD_DIM])
-        )
-        mk_squares = const.tile([mem_rows, HEAD_DIM], F32)
-        mk_sum = const.tile([mem_rows, 1], F32)
-        nc.scalar.activation(out=mk_squares[:], in_=mk[:], func=ACT.Square, accum_out=mk_sum[:])
-        mk_excess = const.tile([mem_rows, 1], F32)
-        nc.scalar.activation(
-            out=mk_excess[:], in_=mk_sum[:], func=ACT.Relu, bias=minus_floor[0:mem_rows]
-        )
+        identity = const.tile([P, P], F32)
+        make_identity(nc, identity[:])
 
-        def finish_memory_rows():
-            mk_rnorm = const.tile([mem_rows, 1], F32)
-            nc.scalar.activation(
-                out=mk_rnorm[:],
-                in_=mk_excess[:],
-                func=ACT.Abs_reciprocal_sqrt,
-                bias=floor[0:mem_rows],
+        w_grouped = const.tile([P, PASS_COLS, 4], BF16, align_bytes=64)
+        w_codes = const.tile([P, PASS_COLS], U32, align_bytes=64)
+        w_scales = const.tile([P, PASS_COLS], U8, align_bytes=64)
+        nc.vector.memset(w_grouped[:].bitcast(I32)[:, COLS:PASS_COLS, :], 0)
+
+        def quantise_weights():
+            dst = w_grouped[:, 0:COLS, :].rearrange("p (a w h i) t -> p a w h i t", a=2, w=3, h=HEADS)
+            for w in range(3):
+                src = w_rows[:, w].rearrange("p t (h a i) -> p a h i t", h=HEADS, a=2)
+                for a in range(2):
+                    nc.vector.tensor_copy(out=dst[:, a, w], in_=src[:, a])
+            nc.vector.quantize_mx(
+                out=w_codes[:].bitcast(FP8X4),
+                scales=w_scales[:],
+                in_=w_grouped[:].rearrange("p c t -> p (c t)"),
             )
-            mk_out = const.tile([mem_rows, BATCH, HEAD_DIM], F32)
-            nc.scalar.activation(
-                out=mk_out[:],
-                in_=mk[:].unsqueeze(1).to_broadcast([mem_rows, BATCH, HEAD_DIM]),
-                func=ACT.Copy,
-                scale=mk_rnorm[:],
-            )
-            for h in range(HEADS):
-                slots = slice(h * MEM, (h + 1) * MEM)
-                nc.sync.dma_start(
-                    out=out_1[:, h, 0:MEM, :].rearrange("b m d -> m b d"), in_=mk_out[slots]
-                )
-                nc.sync.dma_start(
-                    out=out_2[:, h, 0:MEM, :].rearrange("b m d -> m b d"), in_=mv_out[slots]
-                )
-
-        w_codes, w_scales = quantise_weights(nc, const, w_rows)
 
         table = const.tile([P, ROW_TILES, 4, HALF], F32)
+        half_sines = const.tile([P, ROW_TILES, 2, HALF], F32)
+        half_sines_squared = const.tile([P, ROW_TILES, 2, HALF], F32)
 
-        grouped_of, codes_of, scales_of = {}, {}, {}
-        sums_of, excess_of, rnorm_of = {}, {}, {}
-        squares_of, products_of, result_of = {}, {}, {}
-
-        def table_rows(g):
+        def sines(g):
             js = slice(g * GROUP, (g + 1) * GROUP)
-            half_sine = scratch.tile([P, GROUP, 2, HALF], F32)
-            nc.scalar.activation(out=half_sine[:], in_=angle[:, js], func=ACT.Sin, scale=0.5)
+            nc.scalar.activation(out=half_sines[:, js], in_=angle[:, js], func=ACT.Sin, scale=0.5)
             nc.scalar.activation(
                 out=table[:, js, 1, :], in_=angle[:, js, 1, :], func=ACT.Sin, scale=1.0
             )
             nc.scalar.activation(
                 out=table[:, js, 2, :], in_=angle[:, js, 0, :], func=ACT.Sin, scale=-1.0
             )
-            half_sine_squared = scratch.tile([P, GROUP, 2, HALF], F32)
-            nc.gpsimd.tensor_tensor(
-                out=half_sine_squared[:], in0=half_sine[:], in1=half_sine[:], op=ALU.mult
-            )
-            nc.gpsimd.tensor_scalar(
-                out=table[:, js, 0:4:3, :],
-                in0=half_sine_squared[:],
-                scalar1=-2.0,
-                scalar2=1.0,
-                op0=ALU.mult,
-                op1=ALU.add,
-            )
 
-        def prepare(g):
-            x_words = x_groups[g][:].bitcast(F32)
-            grouped = quant.tile([P, GROUP, P, 4], BF16, align_bytes=64)
-            grouped_of[g] = grouped
-            grouped_words = grouped[:].bitcast(F32)
-            for pair in range(GROUP // 2):
-                xt = psum_xt.tile([P, 2, 2, P], F32)
-                for s in range(2):
-                    for u in range(2):
-                        nc.tensor.transpose(
-                            out=xt[:, s, u, :],
-                            in_=x_words[:, 2 * pair + s, u : 2 * P : 2],
-                            identity=identity[:],
-                        )
-                nc.scalar.copy(
-                    out=grouped_words[:, 2 * pair : 2 * pair + 2],
-                    in_=xt[:].rearrange("p s u r -> p s r u"),
+        def cosines(g):
+            js = slice(g * GROUP, (g + 1) * GROUP)
+            if g == 0:
+                nc.scalar.activation(
+                    out=half_sines_squared[:, js], in_=half_sines[:, js], func=ACT.Square
+                )
+                nc.scalar.activation(
+                    out=table[:, js, 0:4:3, :],
+                    in_=half_sines_squared[:, js],
+                    func=ACT.Copy,
+                    scale=-2.0,
+                    bias=1.0,
+                )
+            else:
+                nc.gpsimd.tensor_tensor(
+                    out=half_sines_squared[:, js],
+                    in0=half_sines[:, js],
+                    in1=half_sines[:, js],
+                    op=ALU.mult,
+                )
+                nc.gpsimd.tensor_scalar(
+                    out=table[:, js, 0:4:3, :],
+                    in0=half_sines_squared[:, js],
+                    scalar1=-2.0,
+                    scalar2=1.0,
+                    op0=ALU.mult,
+                    op1=ALU.add,
                 )
 
-        def quantise(g):
-            x_codes = quant.tile([P, GROUP * P], U32, align_bytes=64)
-            x_scales = quant.tile([P, GROUP * P], U8, align_bytes=64)
-            codes_of[g], scales_of[g] = x_codes, x_scales
-            nc.vector.quantize_mx(
-                out=x_codes[:].bitcast(FP8X4),
-                scales=x_scales[:],
-                in_=grouped_of[g][:].rearrange("p s r t -> p (s r t)"),
+        xt_of, grouped_of, codes_of, scales_of, t_of = {}, {}, {}, {}, {}
+        squares_of, eighths_of, sums_of, excess_of, rnorm_of = {}, {}, {}, {}, {}
+        products_of, result_of = {}, {}
+
+        def transpose(i):
+            g, half = divmod(i, 2)
+            x_words = x_groups[g][:].bitcast(F32)
+            xt = psum_xt.tile([P, PAIR, 2, P], F32)
+            xt_of[i] = xt
+            for s in range(PAIR):
+                for u in range(2):
+                    nc.tensor.transpose(
+                        out=xt[:, s, u, :],
+                        in_=x_words[:, PAIR * half + s, u : 2 * P : 2],
+                        identity=identity[:],
+                    )
+
+        def copy_out(i):
+            g, half = divmod(i, 2)
+            if half == 0:
+                grouped = quant.tile([P, GROUP, P, 4], BF16, align_bytes=64)
+                grouped_of[g] = grouped
+            nc.scalar.copy(
+                out=grouped_of[g][:].bitcast(F32)[:, PAIR * half : PAIR * (half + 1)],
+                in_=xt_of[i][:].rearrange("p s u r -> p s r u"),
             )
 
-        def open_group(g):
-            squares = scratch.tile([P, GROUP, NORMED, 2, HALF], F32)
-            sums = norms.tile([P, GROUP, NORMED], F32)
-            products = products_pool.tile([P, GROUP, 2 * COLS], F32)
-            result = result_pool.tile([P, HEAD_GROUPS, GROUP, HEAD_DIM], F32)
-            squares_of[g], sums_of[g], products_of[g], result_of[g] = squares, sums, products, result
+        def quantise(g, first, tiles):
+            if first == 0:
+                x_codes = quant.tile([P, GROUP * P], U32, align_bytes=64)
+                x_scales = quant.tile([P, GROUP * P], U8, align_bytes=64)
+                codes_of[g], scales_of[g] = x_codes, x_scales
+            cols = slice(first * P, (first + tiles) * P)
+            nc.vector.quantize_mx(
+                out=codes_of[g][:, cols].bitcast(FP8X4),
+                scales=scales_of[g][:, cols],
+                in_=grouped_of[g][:, first : first + tiles].rearrange("p s r t -> p (s r t)"),
+            )
 
         def project(g, s):
             tokens = slice(s * P, (s + 1) * P)
             t_psum = psum_t.tile([P, PASS_COLS], F32)
+            t_of[g, s] = t_psum
             nc.tensor.matmul_mx(
                 out=t_psum[:],
                 lhsT=codes_of[g][:, tokens].bitcast(FP8X4),
@@ -213,23 +199,87 @@ def tile_attention_pa_t_kernel(
                 start=True,
                 stop=True,
             )
-            t_halves = t_psum[:, 0:COLS].rearrange("p (a g i) -> p a g i", a=2, g=HEAD_GROUPS)
-            for n in range(NORMED):
-                nc.scalar.activation(
-                    out=squares_of[g][:, s, n],
-                    in_=t_halves[:, :, n, :],
-                    func=ACT.Square,
-                    accum_out=sums_of[g][:, s, n : n + 1],
-                )
+
+        def halves(g, s):
+            return t_of[g, s][:, 0:COLS].rearrange("p (a g i) -> p a g i", a=2, g=HEAD_GROUPS)
+
+        def open_group(g):
+            products = products_pool.tile([P, GROUP, 2 * COLS], F32)
+            result = result_pool.tile([P, HEAD_GROUPS, GROUP, HEAD_DIM], F32)
+            squares = scratch.tile([P, FOLD, GROUP, NORMED * HEAD_DIM // FOLD], F32)
+            products_of[g], result_of[g], squares_of[g] = products, result, squares
+
+        def multiply(g, s):
             j = (g % GROUPS_PER_BATCH) * GROUP + s
             shape = [P, 2, 2, HEAD_GROUPS, HALF]
             nc.vector.tensor_tensor(
                 out=products_of[g][:, s, :].rearrange(
                     "p (a r g i) -> p a r g i", a=2, r=2, g=HEAD_GROUPS
                 ),
-                in0=t_halves.unsqueeze(2).to_broadcast(shape),
+                in0=halves(g, s).unsqueeze(2).to_broadcast(shape),
                 in1=table[:, j].rearrange("p (a r) i -> p a r i", a=2).unsqueeze(3).to_broadcast(shape),
                 op=ALU.mult,
+            )
+
+        def square(g, s):
+            nc.scalar.activation(
+                out=squares_of[g][:, :, s, :].rearrange("p b (a n j) -> p b a n j", a=2, n=NORMED),
+                in_=halves(g, s)[:, :, 0:NORMED, :].rearrange("p a n (j b) -> p b a n j", b=FOLD),
+                func=ACT.Square,
+            )
+
+        indicator = const.tile([P, GROUP, NORMED], F32)
+
+        def make_indicator():
+            nc.vector.tensor_reduce(
+                out=indicator[:],
+                in_=identity[:].rearrange("p (s a n j) -> p s n a j", s=GROUP, a=2, n=NORMED),
+                axis=AXES.XY,
+                op=ALU.add,
+            )
+
+        def fold_squares(g):
+            sums = psum_sum.tile([P, 512], F32)
+            sums_of[g] = sums
+            for b in range(FOLD):
+                nc.tensor.matmul(
+                    out=sums[:, 0:P],
+                    lhsT=squares_of[g][:, b].rearrange("p s m -> p (s m)"),
+                    rhs=identity[:],
+                    start=b == 0,
+                    stop=b == FOLD - 1,
+                    is_transpose=True,
+                )
+
+        def copy_folded(g):
+            folded = norms.tile([P, P], F32)
+            eighths_of[g] = folded
+            nc.scalar.copy(out=folded[:], in_=sums_of[g][:, 0:P])
+
+        def finish_sums(g):
+            nc.tensor.matmul(
+                out=sums_of[g][:, P : P + GROUP * NORMED],
+                lhsT=eighths_of[g][:],
+                rhs=indicator[:].rearrange("p s n -> p (s n)"),
+                start=True,
+                stop=True,
+            )
+
+        def clamp_sums(g):
+            excess = norms.tile([P, GROUP * NORMED], F32)
+            excess_of[g] = excess
+            nc.scalar.activation(
+                out=excess[:],
+                in_=sums_of[g][:, P : P + GROUP * NORMED],
+                func=ACT.Relu,
+                bias=minus_floor[:],
+            )
+
+        def root_sums(g):
+            rnorm = norms.tile([P, GROUP * NORMED], F32)
+            rnorm_of[g] = rnorm
+            nc.scalar.activation(
+                out=rnorm[:], in_=excess_of[g][:], func=ACT.Abs_reciprocal_sqrt, bias=floor[:]
             )
 
         def add_products(engine, g, tiles):
@@ -243,70 +293,139 @@ def tile_attention_pa_t_kernel(
                 op=ALU.add,
             )
 
-        def clamp_sums(g):
-            excess = norms.tile([P, GROUP, NORMED], F32)
-            excess_of[g] = excess
-            nc.scalar.activation(
-                out=excess[:], in_=sums_of[g][:], func=ACT.Relu, bias=minus_floor[:]
-            )
-
-        def root_sums(g):
-            rnorm = norms.tile([P, GROUP, NORMED], F32)
-            rnorm_of[g] = rnorm
-            nc.scalar.activation(
-                out=rnorm[:], in_=excess_of[g][:], func=ACT.Abs_reciprocal_sqrt, bias=floor[:]
-            )
-
         def normalise(g, s):
             for n in range(NORMED):
                 nc.scalar.activation(
                     out=result_of[g][:, n, s, :],
                     in_=result_of[g][:, n, s, :],
                     func=ACT.Copy,
-                    scale=rnorm_of[g][:, s, n : n + 1],
+                    scale=rnorm_of[g][:, s * NORMED + n : s * NORMED + n + 1],
                 )
 
-        def store(g):
+        outs = [out_0, out_1[:, :, MEM:, :], out_2[:, :, MEM:, :]]
+
+        def store(g, w):
             b, j0 = g // GROUPS_PER_BATCH, (g % GROUPS_PER_BATCH) * GROUP
-            out_rows = [out_0[b], out_1[b, :, MEM:, :], out_2[b, :, MEM:, :]]
-            for w in range(3):
-                nc.sync.dma_start(
-                    out=out_rows[w].rearrange("h (p j) d -> p h j d", j=ROW_TILES)[
-                        :, :, j0 : j0 + GROUP, :
-                    ],
-                    in_=result_of[g][:, w * HEADS : (w + 1) * HEADS],
-                )
+            nc.sync.dma_start(
+                out=outs[w][b].rearrange("h (p j) d -> p h j d", j=ROW_TILES)[
+                    :, :, j0 : j0 + GROUP, :
+                ],
+                in_=result_of[g][:, w * HEADS : (w + 1) * HEADS],
+            )
+
+        def memory_rows():
+            mv_out = const.tile([mem_rows, HEAD_DIM], F32)
+            nc.gpsimd.tensor_copy(out=mv_out[:], in_=mv[:])
+            mk_squares = const.tile([mem_rows, HEAD_DIM], F32)
+            mk_sum = const.tile([mem_rows, 1], F32)
+            nc.scalar.activation(out=mk_squares[:], in_=mk[:], func=ACT.Square, accum_out=mk_sum[:])
+            mk_excess = const.tile([mem_rows, 1], F32)
+            nc.scalar.activation(
+                out=mk_excess[:], in_=mk_sum[:], func=ACT.Relu, bias=minus_floor[0:mem_rows]
+            )
+            mk_rnorm = const.tile([mem_rows, 1], F32)
+            nc.scalar.activation(
+                out=mk_rnorm[:],
+                in_=mk_excess[:],
+                func=ACT.Abs_reciprocal_sqrt,
+                bias=floor[0:mem_rows],
+            )
+            mk_out = const.tile([mem_rows, HEAD_DIM], F32)
+            nc.scalar.activation(out=mk_out[:], in_=mk[:], func=ACT.Copy, scale=mk_rnorm[:])
+            for h in range(HEADS):
+                slots = slice(h * MEM, (h + 1) * MEM)
+                for rows, out in [(mk_out, out_1), (mv_out, out_2)]:
+                    nc.sync.dma_start(
+                        out=out[:, h, 0:MEM, :].rearrange("b m d -> m b d"),
+                        in_=rows[slots].unsqueeze(1).to_broadcast([MEM, BATCH, HEAD_DIM]),
+                    )
 
         def live(g):
             return 0 <= g < N_GROUPS
 
-        def pipeline_step(step):
-            if live(step - NORMALISE_BEHIND):
-                root_sums(step - NORMALISE_BEHIND)
-            if live(step + QUANTISE_AHEAD):
-                quantise(step + QUANTISE_AHEAD)
-            if live(step + PREPARE_AHEAD):
-                if step + PREPARE_AHEAD < GROUPS_PER_BATCH:
-                    table_rows(step + PREPARE_AHEAD)
-                prepare(step + PREPARE_AHEAD)
-            if live(step):
-                open_group(step)
+        def step(g):
+            quantise_at = 2 if g == 0 else 0
+            projected = 0
+            if live(g):
+                open_group(g)
+            if live(g + 2):
+                copy_out(2 * g + 4)
+            if live(g - 1):
+                fold_squares(g - 1)
+            if live(g + 3):
+                transpose(2 * g + 6)
+            if live(g - 2):
+                normalise(g - 2, 0)
+                normalise(g - 2, 1)
+            if live(g - 1):
+                copy_folded(g - 1)
             for s in range(GROUP):
-                if live(step):
-                    project(step, s)
-                    if step == N_GROUPS - 1 and s % 2 == 1:
-                        add_products(nc.vector, step, slice(s - 1, s + 1))
-                if live(step - NORMALISE_BEHIND):
-                    normalise(step - NORMALISE_BEHIND, s)
-            if live(step):
-                clamp_sums(step)
-                if step < N_GROUPS - 1:
-                    add_products(nc.gpsimd, step, slice(0, GROUP))
-            if live(step - NORMALISE_BEHIND):
-                store(step - NORMALISE_BEHIND)
+                if live(g + 1):
+                    if s == quantise_at:
+                        quantise(g + 1, 0, GROUP)
+                    if s >= quantise_at:
+                        for t in range(projected, s + 1):
+                            project(g + 1, t)
+                        projected = s + 1
+                if live(g):
+                    multiply(g, s)
+                    square(g, s)
+                if s == 0:
+                    if live(g - 1):
+                        finish_sums(g - 1)
+                    if live(g + 2):
+                        copy_out(2 * g + 5)
+                if s == 1:
+                    if live(g + 3):
+                        transpose(2 * g + 7)
+                    if live(g - 1):
+                        clamp_sums(g - 1)
+                    if live(g - 2):
+                        normalise(g - 2, 2)
+                if s == 2:
+                    if live(g - 1):
+                        root_sums(g - 1)
+                    if live(g - 2):
+                        normalise(g - 2, 3)
+            if live(g):
+                if g < N_GROUPS - 1:
+                    add_products(nc.gpsimd, g, slice(0, GROUP))
+                else:
+                    for s in range(GROUP):
+                        add_products(nc.vector, g, slice(s, s + 1))
+                store(g, 2)
+            if live(g - 2):
+                store(g - 2, 0)
+                store(g - 2, 1)
 
-        for step in range(-PREPARE_AHEAD, NORMALISE_BEHIND):
-            pipeline_step(step)
-        finish_memory_rows()
-        for step in range(NORMALISE_BEHIND, N_GROUPS + NORMALISE_BEHIND):
-            pipeline_step(step)
+        sines(0)
+        quantise_weights()
+        transpose(0)
+        copy_out(0)
+        cosines(0)
+        transpose(1)
+        quantise(0, 0, PAIR)
+        copy_out(1)
+        for s in range(PAIR):
+            project(0, s)
+        quantise(0, PAIR, PAIR)
+        make_indicator()
+        transpose(2)
+        copy_out(2)
+        for s in range(PAIR, GROUP):
+            project(0, s)
+        sines(1)
+        cosines(1)
+        transpose(3)
+        copy_out(3)
+        sines(2)
+        cosines(2)
+        sines(3)
+        cosines(3)
+        transpose(4)
+        transpose(5)
+        step(0)
+        step(1)
+        memory_rows()
+        for g in range(2, N_GROUPS + 2):
+            step(g)

from contextlib import ExitStack

import concourse.mybir as mybir
from concourse.masks import make_identity

F32 = mybir.dt.float32
BF16 = mybir.dt.bfloat16
I32 = mybir.dt.int32
U32 = mybir.dt.uint32
U8 = mybir.dt.uint8
FP8X4 = mybir.dt.float8_e4m3fn_x4
ACT = mybir.ActivationFunctionType
ALU = mybir.AluOpType
AXES = mybir.AxisListType

P = 128
BATCH, TOKENS, DIM = 4, 2048, 512
HEADS, HEAD_DIM, MEM = 2, 64, 16
HALF = HEAD_DIM // 2
HEAD_GROUPS = 3 * HEADS
NORMED = 2 * HEADS
COLS = HEAD_GROUPS * HEAD_DIM
PASS_COLS = 512
ROW_TILES = TOKENS // P
GROUP = 4
PAIR = 2
GROUPS_PER_BATCH = ROW_TILES // GROUP
N_GROUPS = BATCH * GROUPS_PER_BATCH
FOLD = 8
EPS = 1e-12

FLOPS = 2 * BATCH * TOKENS * DIM * COLS


def tile_attention_pa_t_kernel(
    tc, x, freqs, Wq, Wk, Wv, mem_k, mem_v, out_0, out_1, out_2
):
    nc = tc.nc
    with ExitStack() as ctx:
        ctx.enter_context(tc.manual_schedule())
        const = ctx.enter_context(tc.tile_pool(name="const", bufs=1))
        x_pool = ctx.enter_context(tc.tile_pool(name="x", bufs=N_GROUPS))
        quant = ctx.enter_context(tc.tile_pool(name="quant", bufs=3))
        norms = ctx.enter_context(tc.tile_pool(name="norms", bufs=4))
        scratch = ctx.enter_context(tc.tile_pool(name="scratch", bufs=2))
        products_pool = ctx.enter_context(tc.tile_pool(name="products", bufs=3))
        result_pool = ctx.enter_context(tc.tile_pool(name="result", bufs=6))
        psum_xt = ctx.enter_context(tc.psum_pool(name="psum_xt", bufs=2))
        psum_t = ctx.enter_context(tc.psum_pool(name="psum_t", bufs=5))
        psum_sum = ctx.enter_context(tc.psum_pool(name="psum_sum", bufs=1))

        w_rows = const.tile([P, 3, 4, P], BF16)
        for w, weight in enumerate([Wq, Wk, Wv]):
            nc.sync.dma_start(out=w_rows[:, w], in_=weight.rearrange("(p t) c -> p t c", t=4))
        angle = const.tile([P, ROW_TILES, 2, HALF], BF16)
        mem_rows = HEADS * MEM
        mk = const.tile([mem_rows, HEAD_DIM], BF16)
        mv = const.tile([mem_rows, HEAD_DIM], BF16)
        x_groups = []
        for g in range(N_GROUPS):
            b, j0 = g // GROUPS_PER_BATCH, (g % GROUPS_PER_BATCH) * GROUP
            x_rows = x[b].rearrange("(p j) k -> p j k", j=ROW_TILES)
            x_group = x_pool.tile([P, GROUP, DIM], BF16)
            x_groups.append(x_group)
            width = PAIR if g == 0 else GROUP
            for c in range(0, GROUP, width):
                nc.sync.dma_start(
                    out=x_group[:, c : c + width], in_=x_rows[:, j0 + c : j0 + c + width, :]
                )
                if g == 0 and c == 0:
                    nc.sync.dma_start(
                        out=angle[:],
                        in_=freqs.rearrange("(p j) (s i) -> p j s i", j=ROW_TILES, s=2),
                    )
            if g == 1:
                nc.sync.dma_start(out=mk[:], in_=mem_k.rearrange("h m d -> (h m) d"))
                nc.sync.dma_start(out=mv[:], in_=mem_v.rearrange("h m d -> (h m) d"))

        floor = const.tile([P, 1], F32)
        nc.vector.memset(floor[:], EPS * EPS)
        minus_floor = const.tile([P, 1], F32)
        nc.vector.memset(minus_floor[:], -EPS * EPS)
        warm = const.tile([P, 2], F32)
        nc.vector.memset(warm[:], 1.0)
        nc.scalar.activation(out=warm[:, 0:1], in_=warm[:, 1:2], func=ACT.Sin)

        identity = const.tile([P, P], F32)
        make_identity(nc, identity[:])

        w_grouped = const.tile([P, PASS_COLS, 4], BF16, align_bytes=64)
        w_codes = const.tile([P, PASS_COLS], U32, align_bytes=64)
        w_scales = const.tile([P, PASS_COLS], U8, align_bytes=64)
        nc.vector.memset(w_grouped[:].bitcast(I32)[:, COLS:PASS_COLS, :], 0)

        def quantise_weights():
            dst = w_grouped[:, 0:COLS, :].rearrange("p (a w h i) t -> p a w h i t", a=2, w=3, h=HEADS)
            for w in range(3):
                src = w_rows[:, w].rearrange("p t (h a i) -> p a h i t", h=HEADS, a=2)
                for a in range(2):
                    nc.vector.tensor_copy(out=dst[:, a, w], in_=src[:, a])
            nc.vector.quantize_mx(
                out=w_codes[:].bitcast(FP8X4),
                scales=w_scales[:],
                in_=w_grouped[:].rearrange("p c t -> p (c t)"),
            )

        table = const.tile([P, ROW_TILES, 4, HALF], F32)
        half_sines = const.tile([P, ROW_TILES, 2, HALF], F32)
        half_sines_squared = const.tile([P, ROW_TILES, 2, HALF], F32)

        def sines(g):
            js = slice(g * GROUP, (g + 1) * GROUP)
            nc.scalar.activation(out=half_sines[:, js], in_=angle[:, js], func=ACT.Sin, scale=0.5)
            nc.scalar.activation(
                out=table[:, js, 1, :], in_=angle[:, js, 1, :], func=ACT.Sin, scale=1.0
            )
            nc.scalar.activation(
                out=table[:, js, 2, :], in_=angle[:, js, 0, :], func=ACT.Sin, scale=-1.0
            )

        def cosines(g):
            js = slice(g * GROUP, (g + 1) * GROUP)
            if g == 0:
                nc.scalar.activation(
                    out=half_sines_squared[:, js], in_=half_sines[:, js], func=ACT.Square
                )
                nc.scalar.activation(
                    out=table[:, js, 0:4:3, :],
                    in_=half_sines_squared[:, js],
                    func=ACT.Copy,
                    scale=-2.0,
                    bias=1.0,
                )
            else:
                nc.gpsimd.tensor_tensor(
                    out=half_sines_squared[:, js],
                    in0=half_sines[:, js],
                    in1=half_sines[:, js],
                    op=ALU.mult,
                )
                nc.gpsimd.tensor_scalar(
                    out=table[:, js, 0:4:3, :],
                    in0=half_sines_squared[:, js],
                    scalar1=-2.0,
                    scalar2=1.0,
                    op0=ALU.mult,
                    op1=ALU.add,
                )

        xt_of, grouped_of, codes_of, scales_of, t_of = {}, {}, {}, {}, {}
        squares_of, eighths_of, sums_of, excess_of, rnorm_of = {}, {}, {}, {}, {}
        products_of, result_of = {}, {}

        def transpose(i):
            g, half = divmod(i, 2)
            x_words = x_groups[g][:].bitcast(F32)
            xt = psum_xt.tile([P, PAIR, 2, P], F32)
            xt_of[i] = xt
            for s in range(PAIR):
                for u in range(2):
                    nc.tensor.transpose(
                        out=xt[:, s, u, :],
                        in_=x_words[:, PAIR * half + s, u : 2 * P : 2],
                        identity=identity[:],
                    )

        def copy_out(i):
            g, half = divmod(i, 2)
            if half == 0:
                grouped = quant.tile([P, GROUP, P, 4], BF16, align_bytes=64)
                grouped_of[g] = grouped
            nc.scalar.copy(
                out=grouped_of[g][:].bitcast(F32)[:, PAIR * half : PAIR * (half + 1)],
                in_=xt_of[i][:].rearrange("p s u r -> p s r u"),
            )

        def quantise(g, first, tiles):
            if first == 0:
                x_codes = quant.tile([P, GROUP * P], U32, align_bytes=64)
                x_scales = quant.tile([P, GROUP * P], U8, align_bytes=64)
                codes_of[g], scales_of[g] = x_codes, x_scales
            cols = slice(first * P, (first + tiles) * P)
            nc.vector.quantize_mx(
                out=codes_of[g][:, cols].bitcast(FP8X4),
                scales=scales_of[g][:, cols],
                in_=grouped_of[g][:, first : first + tiles].rearrange("p s r t -> p (s r t)"),
            )

        def project(g, s):
            tokens = slice(s * P, (s + 1) * P)
            t_psum = psum_t.tile([P, PASS_COLS], F32)
            t_of[g, s] = t_psum
            nc.tensor.matmul_mx(
                out=t_psum[:],
                lhsT=codes_of[g][:, tokens].bitcast(FP8X4),
                lhsT_scale=scales_of[g][:, tokens],
                rhs=w_codes[:].bitcast(FP8X4),
                rhs_scale=w_scales[:],
                start=True,
                stop=True,
            )

        def halves(g, s):
            return t_of[g, s][:, 0:COLS].rearrange("p (a g i) -> p a g i", a=2, g=HEAD_GROUPS)

        def open_group(g):
            products = products_pool.tile([P, GROUP, 2 * COLS], F32)
            result = result_pool.tile([P, HEAD_GROUPS, GROUP, HEAD_DIM], F32)
            squares = scratch.tile([P, FOLD, GROUP, NORMED * HEAD_DIM // FOLD], F32)
            products_of[g], result_of[g], squares_of[g] = products, result, squares

        def multiply(g, s):
            j = (g % GROUPS_PER_BATCH) * GROUP + s
            shape = [P, 2, 2, HEAD_GROUPS, HALF]
            nc.vector.tensor_tensor(
                out=products_of[g][:, s, :].rearrange(
                    "p (a r g i) -> p a r g i", a=2, r=2, g=HEAD_GROUPS
                ),
                in0=halves(g, s).unsqueeze(2).to_broadcast(shape),
                in1=table[:, j].rearrange("p (a r) i -> p a r i", a=2).unsqueeze(3).to_broadcast(shape),
                op=ALU.mult,
            )

        def square(g, s):
            nc.scalar.activation(
                out=squares_of[g][:, :, s, :].rearrange("p b (a n j) -> p b a n j", a=2, n=NORMED),
                in_=halves(g, s)[:, :, 0:NORMED, :].rearrange("p a n (j b) -> p b a n j", b=FOLD),
                func=ACT.Square,
            )

        indicator = const.tile([P, GROUP, NORMED], F32)

        def make_indicator():
            nc.vector.tensor_reduce(
                out=indicator[:],
                in_=identity[:].rearrange("p (s a n j) -> p s n a j", s=GROUP, a=2, n=NORMED),
                axis=AXES.XY,
                op=ALU.add,
            )

        def fold_squares(g):
            sums = psum_sum.tile([P, 512], F32)
            sums_of[g] = sums
            for b in range(FOLD):
                nc.tensor.matmul(
                    out=sums[:, 0:P],
                    lhsT=squares_of[g][:, b].rearrange("p s m -> p (s m)"),
                    rhs=identity[:],
                    start=b == 0,
                    stop=b == FOLD - 1,
                    is_transpose=True,
                )

        def copy_folded(g):
            folded = norms.tile([P, P], F32)
            eighths_of[g] = folded
            nc.scalar.copy(out=folded[:], in_=sums_of[g][:, 0:P])

        def finish_sums(g):
            nc.tensor.matmul(
                out=sums_of[g][:, P : P + GROUP * NORMED],
                lhsT=eighths_of[g][:],
                rhs=indicator[:].rearrange("p s n -> p (s n)"),
                start=True,
                stop=True,
            )

        def clamp_sums(g):
            excess = norms.tile([P, GROUP * NORMED], F32)
            excess_of[g] = excess
            nc.scalar.activation(
                out=excess[:],
                in_=sums_of[g][:, P : P + GROUP * NORMED],
                func=ACT.Relu,
                bias=minus_floor[:],
            )

        def root_sums(g):
            rnorm = norms.tile([P, GROUP * NORMED], F32)
            rnorm_of[g] = rnorm
            nc.scalar.activation(
                out=rnorm[:], in_=excess_of[g][:], func=ACT.Abs_reciprocal_sqrt, bias=floor[:]
            )

        def add_products(engine, g, tiles):
            by_source = products_of[g][:, tiles, :].rearrange(
                "p s (a r g i) -> p a s r g i", a=2, r=2, g=HEAD_GROUPS
            )
            engine.tensor_tensor(
                out=result_of[g][:, :, tiles, :].rearrange("p g s (r i) -> p s r g i", r=2),
                in0=by_source[:, 0],
                in1=by_source[:, 1],
                op=ALU.add,
            )

        def normalise(g, s):
            for n in range(NORMED):
                nc.scalar.activation(
                    out=result_of[g][:, n, s, :],
                    in_=result_of[g][:, n, s, :],
                    func=ACT.Copy,
                    scale=rnorm_of[g][:, s * NORMED + n : s * NORMED + n + 1],
                )

        outs = [out_0, out_1[:, :, MEM:, :], out_2[:, :, MEM:, :]]

        def store(g, w):
            b, j0 = g // GROUPS_PER_BATCH, (g % GROUPS_PER_BATCH) * GROUP
            nc.sync.dma_start(
                out=outs[w][b].rearrange("h (p j) d -> p h j d", j=ROW_TILES)[
                    :, :, j0 : j0 + GROUP, :
                ],
                in_=result_of[g][:, w * HEADS : (w + 1) * HEADS],
            )

        def memory_rows():
            mv_out = const.tile([mem_rows, HEAD_DIM], F32)
            nc.gpsimd.tensor_copy(out=mv_out[:], in_=mv[:])
            mk_squares = const.tile([mem_rows, HEAD_DIM], F32)
            mk_sum = const.tile([mem_rows, 1], F32)
            nc.scalar.activation(out=mk_squares[:], in_=mk[:], func=ACT.Square, accum_out=mk_sum[:])
            mk_excess = const.tile([mem_rows, 1], F32)
            nc.scalar.activation(
                out=mk_excess[:], in_=mk_sum[:], func=ACT.Relu, bias=minus_floor[0:mem_rows]
            )
            mk_rnorm = const.tile([mem_rows, 1], F32)
            nc.scalar.activation(
                out=mk_rnorm[:],
                in_=mk_excess[:],
                func=ACT.Abs_reciprocal_sqrt,
                bias=floor[0:mem_rows],
            )
            mk_out = const.tile([mem_rows, HEAD_DIM], F32)
            nc.scalar.activation(out=mk_out[:], in_=mk[:], func=ACT.Copy, scale=mk_rnorm[:])
            for h in range(HEADS):
                slots = slice(h * MEM, (h + 1) * MEM)
                for rows, out in [(mk_out, out_1), (mv_out, out_2)]:
                    nc.sync.dma_start(
                        out=out[:, h, 0:MEM, :].rearrange("b m d -> m b d"),
                        in_=rows[slots].unsqueeze(1).to_broadcast([MEM, BATCH, HEAD_DIM]),
                    )

        def live(g):
            return 0 <= g < N_GROUPS

        def step(g):
            quantise_at = 2 if g == 0 else 0
            projected = 0
            if live(g):
                open_group(g)
            if live(g + 2):
                copy_out(2 * g + 4)
            if live(g - 1):
                fold_squares(g - 1)
            if live(g + 3):
                transpose(2 * g + 6)
            if live(g - 2):
                normalise(g - 2, 0)
                normalise(g - 2, 1)
            if live(g - 1):
                copy_folded(g - 1)
            for s in range(GROUP):
                if live(g + 1):
                    if s == quantise_at:
                        quantise(g + 1, 0, GROUP)
                    if s >= quantise_at:
                        for t in range(projected, s + 1):
                            project(g + 1, t)
                        projected = s + 1
                if live(g):
                    multiply(g, s)
                    square(g, s)
                if s == 0:
                    if live(g - 1):
                        finish_sums(g - 1)
                    if live(g + 2):
                        copy_out(2 * g + 5)
                if s == 1:
                    if live(g + 3):
                        transpose(2 * g + 7)
                    if live(g - 1):
                        clamp_sums(g - 1)
                    if live(g - 2):
                        normalise(g - 2, 2)
                if s == 2:
                    if live(g - 1):
                        root_sums(g - 1)
                    if live(g - 2):
                        normalise(g - 2, 3)
            if live(g):
                if g < N_GROUPS - 1:
                    add_products(nc.gpsimd, g, slice(0, GROUP))
                else:
                    for s in range(GROUP):
                        add_products(nc.vector, g, slice(s, s + 1))
                store(g, 2)
            if live(g - 2):
                store(g - 2, 0)
                store(g - 2, 1)

        sines(0)
        quantise_weights()
        transpose(0)
        copy_out(0)
        cosines(0)
        transpose(1)
        quantise(0, 0, PAIR)
        copy_out(1)
        for s in range(PAIR):
            project(0, s)
        quantise(0, PAIR, PAIR)
        make_indicator()
        transpose(2)
        copy_out(2)
        for s in range(PAIR, GROUP):
            project(0, s)
        sines(1)
        cosines(1)
        transpose(3)
        copy_out(3)
        sines(2)
        cosines(2)
        sines(3)
        cosines(3)
        transpose(4)
        transpose(5)
        step(0)
        step(1)
        memory_rows()
        for g in range(2, N_GROUPS + 2):
            step(g)
